import numpy as np
import ml_dtypes


def mxq(x, axis, fmt="e4m3"):
    dtype, down = {"e4m3": (ml_dtypes.float8_e4m3fn, 7), "e5m2": (ml_dtypes.float8_e5m2, 14)}[fmt]
    v = np.moveaxis(np.asarray(x, np.float32).astype(ml_dtypes.bfloat16).astype(np.float64), axis, -1)
    blocks = v.reshape(v.shape[:-1] + (-1, 32))
    amax = np.abs(blocks).max(-1, keepdims=True)
    byte = np.maximum(np.where(amax > 0, np.frexp(amax)[1] - 1 + 127, 0) - down, 1)
    scale = np.exp2(byte - 127.0)
    codes = (blocks / scale).astype(np.float32).astype(dtype).astype(np.float64)
    return np.moveaxis((codes * scale).reshape(v.shape), -1, axis)


WIDE = False


def mx_kscale(k):
    if not WIDE:
        return np.ones(k)
    levels = np.array([10, -10, 5, -5, 0])
    if k % 512:
        return np.exp2(np.random.permutation(np.resize(levels, k // 32))).repeat(32)
    a = np.empty((k // 512, 16))
    for p in range(k // 512):
        a[p, :8] = np.random.permutation(np.resize(levels, 8))
        for g in range(8):
            far = levels[np.abs(levels - a[p, g]) >= 10]
            a[p, g + 8] = far[np.random.randint(len(far))]
    return np.exp2(a.ravel()).repeat(32)


BF16 = ml_dtypes.bfloat16


def bf(x):
    return np.asarray(x, np.float32).astype(BF16)


def f64(x):
    return np.asarray(x).astype(np.float64)


NM, B, IN, H1, H2, OUT = 8, 128, 512, 512, 512, 128
LS_LO, LS_HI = -20.0, 4.0


def fnoise(ei, ej):
    return np.sign(ei) * np.sign(ej) * np.sqrt(np.abs(ei)) * np.sqrt(np.abs(ej))


def plin(xq, w, b):
    y = xq.transpose(1, 0, 2) @ mxq(f64(w), 2, 'e4m3').transpose(0, 2, 1)
    return y.transpose(1, 0, 2) + f64(b)[None]


def setup_inputs():
    k = mx_kscale(IN)
    return {'s': bf(np.random.standard_normal((B, NM, IN)) * k),
            'ei1': bf(np.random.standard_normal((B, NM, 1))),
            'ej1': bf(np.random.standard_normal((1, NM, H1))),
            'w11': bf(np.random.standard_normal((NM, H1, IN)) / np.sqrt(IN) / k),
            'b11': bf(np.random.standard_normal((NM, H1)) * 0.3),
            'w12': bf(np.random.standard_normal((NM, H1, IN)) * 1.2 / np.sqrt(IN) / k),
            'b12': bf(np.random.standard_normal((NM, H1)) * 0.3)}


def reference(s, ei1, ej1, w11, b11, w12, b12):
    sq = mxq(f64(s), 2, 'e4m3')
    mu = plin(sq, w11, b11)
    log_sigma = np.clip(plin(sq, w12, b12), LS_LO, LS_HI)
    return np.maximum(mu + fnoise(f64(ei1), f64(ej1)) * np.exp(log_sigma), 0.0)

@@ -1,0 +1,321 @@
+import concourse.mybir as mybir
+from concourse.masks import make_identity
+
+F32 = mybir.dt.float32
+BF16 = mybir.dt.bfloat16
+U32 = mybir.dt.uint32
+U8 = mybir.dt.uint8
+I32 = mybir.dt.int32
+FP8X4 = mybir.dt.float8_e4m3fn_x4
+ALU = mybir.AluOpType
+ACT = mybir.ActivationFunctionType
+
+P = 128
+NM = 8
+K = 512
+H = 512
+NT = H // P
+FLOPS = 2 * 2 * P * NM * K * H
+LS, MU = 1, 0
+
+
+def tile_skill_net_pa_kernel(tc, s, ei1, ej1, w11, b11, w12, b12, out):
+    nc = tc.nc
+    with tc.tile_pool(name="const", bufs=1) as const, tc.tile_pool(name="raw", bufs=1) as raw, tc.tile_pool(
+        name="work", bufs=2
+    ) as work, tc.psum_pool(name="pst", bufs=4) as pst, tc.psum_pool(name="psx", bufs=3) as psx, tc.psum_pool(
+        name="pso", bufs=1
+    ) as pso:
+        vcopy = nc.vector.tensor_copy
+        scopy = nc.scalar.copy
+
+        NJ = NM * NT
+        noise_in = const.tile([P, NJ + NM], BF16)
+        b_sb = {MU: const.tile([P, NJ], BF16, name="b_mu"), LS: const.tile([P, NJ], BF16, name="b_ls")}
+        bounds = const.tile([P, 2], F32)
+        warm = const.tile([P, 1], F32)
+        ident = const.tile([P, P], F32)
+        ebounds = const.tile([P, 2], F32)
+        mag = const.tile([P, NJ + NM], F32)
+        neg = const.tile([P, NJ + NM], F32)
+        sgn = const.tile([P, NJ + NM], F32)
+        root = const.tile([P, NJ + NM], F32)
+        f = const.tile([P, NJ + NM], F32)
+        rep = const.tile([P, NM * P], F32)
+        fi_all = const.tile([P, NM * P], F32)
+        s_codes = const.tile([P, NM * P], U32, align_bytes=64)
+        s_scales = const.tile([P, NM * P], U8, align_bytes=64)
+        s_sb = raw.tile([P, NM * K], BF16)
+        w_dram = {LS: w12, MU: w11}
+        b_dram = {LS: b12, MU: b11}
+        w_sb = {}
+        for j in range(NM):
+            for w in (LS, MU):
+                w_sb[(w, j)] = raw.tile([P, NT * K], BF16, name="w%d_%d" % (w, j))
+
+        banks = {}
+        grouped = {}
+        codes = {}
+        scales = {}
+        acc = {}
+        sb = {}
+
+        def load_w(j):
+            for w in (LS, MU):
+                nc.sync.dma_start(out=w_sb[(w, j)][:], in_=w_dram[w][j].rearrange("(p t) k -> p (t k)", t=NT))
+
+        def load_s(c):
+            s_flat = s.rearrange("i j k -> i (j k)")
+            nc.sync.dma_start(out=s_sb[:, 2 * K * c : 2 * K * (c + 1)], in_=s_flat[:, 2 * K * c : 2 * K * (c + 1)])
+
+        def load_b(w):
+            nc.sync.dma_start(
+                out=b_sb[w][:].rearrange("p (j t) -> p j t", t=NT), in_=b_dram[w].rearrange("j (p t) -> p j t", t=NT)
+            )
+
+        def flip(key, src32, stride):
+            tp = pst.tile([P, 512], F32, tag="tp")
+            for a in range(4):
+                first = P * stride * (a // stride) + a % stride
+                nc.tensor.transpose(
+                    tp[:, P * a : P * a + P], src32[:, first : P * stride * (a // stride + 1) : stride], ident[:]
+                )
+            banks[key] = tp
+
+        def regroup(copy, dst32, key):
+            copy(
+                out=dst32.rearrange("q (a p u) -> q a p u", a=2, u=2),
+                in_=banks[key][:].rearrange("q (a u p) -> q a p u", a=2, u=2),
+            )
+
+        def t_w(j, w, h):
+            flip((w, j, h), w_sb[(w, j)][:].bitcast(F32)[:, 512 * h : 512 * h + 512], 2)
+
+        def e_w(j, w, h, copy):
+            if h == 0:
+                grouped[(w, j)] = work.tile([P, 2048], BF16, align_bytes=64, tag="g", bufs=4, name="g")
+            regroup(copy, grouped[(w, j)][:].bitcast(F32)[:, 512 * h : 512 * h + 512], (w, j, h))
+
+        def q_w(j, w):
+            codes[(w, j)] = work.tile([P, 512], U32, align_bytes=64, tag="cw", bufs=4, name="cw")
+            scales[(w, j)] = work.tile([P, 512], U8, align_bytes=64, tag="sw", bufs=4, name="sw")
+            nc.vector.quantize_mx(
+                out=codes[(w, j)][:].bitcast(FP8X4), scales=scales[(w, j)][:], in_=grouped[(w, j)][:]
+            )
+
+        def t_s(c):
+            flip(("s", c), s_sb[:].bitcast(F32)[:, 512 * c : 512 * c + 512], 2)
+
+        def eq_s(c):
+            g = work.tile([P, 1024], BF16, align_bytes=64, tag="gs", bufs=2)
+            regroup(vcopy, g[:].bitcast(F32), ("s", c))
+            nc.vector.quantize_mx(
+                out=s_codes[:, 256 * c : 256 * c + 256].bitcast(FP8X4),
+                scales=s_scales[:, 256 * c : 256 * c + 256],
+                in_=g[:],
+            )
+
+        def t_f(hh):
+            flip(("f", hh), rep[:, 512 * hh : 512 * hh + 512], 1)
+
+        def e_f(hh):
+            vcopy(out=fi_all[:, 512 * hh : 512 * hh + 512], in_=banks[("f", hh)][:])
+
+        def open_bank(j, w):
+            acc[(w, j)] = psx.tile([P, 512], F32, tag="mx", name="mx")
+
+        def mx(j, w, n_dummy):
+            if (w, j) not in acc:
+                open_bank(j, w)
+            ps = acc[(w, j)]
+            for t in range(NT):
+                nc.tensor.matmul_mx(
+                    out=ps[:, P * t : P * t + P],
+                    lhsT=codes[(w, j)][:, P * t : P * t + P].bitcast(FP8X4),
+                    lhsT_scale=scales[(w, j)][:, P * t : P * t + P],
+                    rhs=s_codes[:, P * j : P * j + P].bitcast(FP8X4),
+                    rhs_scale=s_scales[:, P * j : P * j + P],
+                    start=True,
+                    stop=True,
+                )
+
+        def x_(j):
+            e = work.tile([P, 512], F32, tag="e")
+            for t in range(NT):
+                nc.scalar.activation(
+                    out=e[:, P * t : P * t + P],
+                    in_=acc[(LS, j)][:, P * t : P * t + P],
+                    func=ACT.Exp,
+                    bias=b_sb[LS][:, NT * j + t : NT * j + t + 1],
+                    scale=1.0,
+                )
+            sb[("e", j)] = e
+
+        def czo(j):
+            a_sb = work.tile([P, 512], F32, tag="a")
+            nc.vector.tensor_scalar(
+                out=a_sb[:],
+                in0=sb[("e", j)][:],
+                scalar1=ebounds[:, 0:1],
+                scalar2=ebounds[:, 1:2],
+                op0=ALU.max,
+                op1=ALU.min,
+            )
+            z = work.tile([P, 512], F32, tag="z")
+            o = work.tile([P, 512], F32, tag="o")
+            for t in range(NT):
+                nc.vector.scalar_tensor_tensor(
+                    out=z[:, P * t : P * t + P],
+                    in0=a_sb[:, P * t : P * t + P],
+                    scalar=f[:, NT * j + t : NT * j + t + 1],
+                    in1=fi_all[:, P * j : P * j + P],
+                    op0=ALU.mult,
+                    op1=ALU.mult,
+                )
+            for t in range(NT):
+                nc.vector.scalar_tensor_tensor(
+                    out=o[:, P * t : P * t + P],
+                    in0=acc[(MU, j)][:, P * t : P * t + P],
+                    scalar=b_sb[MU][:, NT * j + t : NT * j + t + 1],
+                    in1=z[:, P * t : P * t + P],
+                    op0=ALU.add,
+                    op1=ALU.add,
+                )
+            sb[("o", j)] = o
+
+        def ot_(j, ot, n_matmul):
+            for t in range(NT):
+                if t < n_matmul:
+                    nc.tensor.matmul(
+                        out=ot[:, P * t : P * t + P],
+                        lhsT=sb[("o", j)][:, P * t : P * t + P],
+                        rhs=ident[:],
+                        start=True,
+                        stop=True,
+                    )
+                else:
+                    nc.tensor.transpose(ot[:, P * t : P * t + P], sb[("o", j)][:, P * t : P * t + P], ident[:])
+            banks[("o", j)] = ot
+
+        def r_(j):
+            r = work.tile([P, 512], F32, tag="r", bufs=3)
+            nc.scalar.activation(
+                out=r[:].rearrange("i (p t) -> i p t", t=NT),
+                in_=banks[("o", j)][:].rearrange("i (t p) -> i p t", t=NT),
+                func=ACT.Relu,
+            )
+            nc.sync.dma_start(out=out[:, j, :], in_=r[:])
+
+        nc.sync.dma_start(
+            out=noise_in[:, 0:NJ].rearrange("p (j t) -> p j t", t=NT),
+            in_=ej1.rearrange("o j (p t) -> p (o j) t", t=NT),
+        )
+        nc.sync.dma_start(out=noise_in[:, NJ : NJ + NM], in_=ei1.rearrange("i j o -> i (j o)"))
+        load_s(0)
+        load_w(0)
+        load_w(1)
+        load_b(LS)
+        load_s(1)
+        load_w(2)
+        load_b(MU)
+        load_s(2)
+        load_w(3)
+        load_s(3)
+        for j in range(4, NM):
+            load_w(j)
+
+        with tc.manual_schedule():
+            make_identity(nc, ident[:])
+            nc.vector.memset(bounds[:, 0:1], -20.0)
+            nc.vector.memset(bounds[:, 1:2], 4.0)
+            nc.scalar.activation(out=warm[:], in_=bounds[:, 1:2], func=ACT.Sqrt)
+
+            nc.vector.scalar_tensor_tensor(
+                out=mag[:], in0=noise_in[:], scalar=-1.0, in1=noise_in[:], op0=ALU.mult, op1=ALU.max
+            )
+            nc.vector.tensor_scalar_max(out=mag[:], in0=mag[:], scalar1=2.0 ** -116)
+            nc.vector.tensor_single_scalar(out=neg[:], in_=noise_in[:], scalar=0.0, op=ALU.is_lt)
+            nc.vector.scalar_tensor_tensor(
+                out=sgn[:], in0=noise_in[:], scalar=0.0, in1=neg[:], op0=ALU.is_gt, op1=ALU.subtract
+            )
+            nc.scalar.activation(out=root[:], in_=mag[:], func=ACT.Sqrt)
+            nc.scalar.activation(out=ebounds[:], in_=bounds[:], func=ACT.Exp)
+            nc.vector.tensor_mul(out=f[:], in0=root[:], in1=sgn[:])
+            nc.gpsimd.tensor_scalar(
+                out=rep[:].rearrange("i (j c) -> i j c", j=NM),
+                in0=f[:, NJ : NJ + NM].unsqueeze(2).to_broadcast([P, NM, P]),
+                scalar1=1.0,
+                scalar2=0.0,
+                op0=ALU.mult,
+                op1=ALU.add,
+            )
+
+        t_s(0)
+        eq_s(0)
+        t_w(0, LS, 0)
+        t_w(0, LS, 1)
+        e_w(0, LS, 0, scopy)
+        e_w(0, LS, 1, vcopy)
+        t_w(0, MU, 0)
+        t_w(0, MU, 1)
+        q_w(0, LS)
+        e_w(0, MU, 0, scopy)
+        e_w(0, MU, 1, vcopy)
+        q_w(0, MU)
+        t_w(1, LS, 0)
+        t_w(1, LS, 1)
+        t_f(0)
+        e_f(0)
+        t_w(1, MU, 0)
+
+        chores = {0: ("s", 1), 1: ("s", 2), 2: ("f", 1), 3: ("s", 3)}
+        for n in range(NM + 2):
+            j = n + 1
+            d = n - 1
+            chore = chores.get(n)
+            if n < NM:
+                mx(n, LS, 0)
+                mx(n, MU, 0)
+            if n == 0:
+                t_w(1, MU, 1)
+            if 0 <= d < NM:
+                czo(d)
+            if j < NM:
+                e_w(j, LS, 0, scopy)
+            if n >= 2:
+                r_(n - 2)
+            if chore:
+                if chore[0] == "s":
+                    t_s(chore[1])
+                else:
+                    t_f(chore[1])
+            if j < NM:
+                e_w(j, LS, 1, scopy)
+            if j + 1 < NM:
+                t_w(j + 1, LS, 0)
+            if chore:
+                if chore[0] == "s":
+                    eq_s(chore[1])
+                else:
+                    e_f(chore[1])
+            if j < NM:
+                q_w(j, LS)
+                e_w(j, MU, 0, scopy)
+            if j + 1 < NM:
+                t_w(j + 1, LS, 1)
+            if j < NM:
+                e_w(j, MU, 1, scopy)
+            if 0 <= d < NM:
+                if d == NM - 1:
+                    last_ot = pst.tile([P, 512], F32, tag="tp")
+                    ot_(d, last_ot, 0)
+                else:
+                    ot = pso.tile([P, 512], F32, tag="ot")
+                    ot_(d, ot, 3)
+            if j + 1 < NM:
+                t_w(j + 1, MU, 0)
+                t_w(j + 1, MU, 1)
+            if j < NM:
+                q_w(j, MU)
+            if n < NM:
+                x_(n)

@@ -311,7 +311,7 @@ def tile_skill_net_pa_kernel(tc, s, ei1, ej1, w11, b11, w12, b12, out):
                     ot_(d, last_ot, 0)
                 else:
                     ot = pso.tile([P, 512], F32, tag="ot")
-                    ot_(d, ot, 3)
+                    ot_(d, ot, 0)
             if j + 1 < NM:
                 t_w(j + 1, MU, 0)
                 t_w(j + 1, MU, 1)

@@ -1,3 +1,5 @@
+import math
+
 import concourse.mybir as mybir
 from concourse.masks import make_identity
 
@@ -30,24 +32,25 @@ def tile_skill_net_pa_kernel(tc, s, ei1, ej1, w11, b11, w12, b12, out):
         scopy = nc.scalar.copy
 
         NJ = NM * NT
-        noise_in = const.tile([P, NJ + NM], BF16)
-        b_sb = {MU: const.tile([P, NJ], BF16, name="b_mu"), LS: const.tile([P, NJ], BF16, name="b_ls")}
-        bounds = const.tile([P, 2], F32)
+        vec_rows = const.tile([P, H], BF16)
+        ei_in = const.tile([P, NM], BF16)
+        vec = const.tile([P, 3 * NJ], F32)
+        noise_in = const.tile([P, NJ + NM], F32)
         warm = const.tile([P, 1], F32)
         ident = const.tile([P, P], F32)
-        ebounds = const.tile([P, 2], F32)
+        ident16 = const.tile([P, P], BF16)
+        iy = const.tile([P, NJ + NM], I32)
+        xyy = const.tile([P, NJ + NM], F32)
         mag = const.tile([P, NJ + NM], F32)
         neg = const.tile([P, NJ + NM], F32)
         sgn = const.tile([P, NJ + NM], F32)
         root = const.tile([P, NJ + NM], F32)
         f = const.tile([P, NJ + NM], F32)
-        rep = const.tile([P, NM * P], F32)
         fi_all = const.tile([P, NM * P], F32)
         s_codes = const.tile([P, NM * P], U32, align_bytes=64)
         s_scales = const.tile([P, NM * P], U8, align_bytes=64)
         s_sb = raw.tile([P, NM * K], BF16)
         w_dram = {LS: w12, MU: w11}
-        b_dram = {LS: b12, MU: b11}
         w_sb = {}
         for j in range(NM):
             for w in (LS, MU):
@@ -60,18 +63,23 @@ def tile_skill_net_pa_kernel(tc, s, ei1, ej1, w11, b11, w12, b12, out):
         acc = {}
         sb = {}
 
-        def load_w(j):
-            for w in (LS, MU):
-                nc.sync.dma_start(out=w_sb[(w, j)][:], in_=w_dram[w][j].rearrange("(p t) k -> p (t k)", t=NT))
+        def load_w(j, w, parts):
+            width = NT * K // parts
+            if parts == 1:
+                nc.sync.dma_start(
+                    out=w_sb[(w, j)][:].rearrange("p (h c) -> p h c", h=2),
+                    in_=w_dram[w][j].rearrange("(h p u) k -> p h (u k)", h=2, u=2),
+                )
+            else:
+                for h in range(2):
+                    nc.sync.dma_start(
+                        out=w_sb[(w, j)][:, width * h : width * (h + 1)],
+                        in_=w_dram[w][j][256 * h : 256 * (h + 1), :].rearrange("(p u) k -> p (u k)", u=2),
+                    )
 
         def load_s(c):
             s_flat = s.rearrange("i j k -> i (j k)")
             nc.sync.dma_start(out=s_sb[:, 2 * K * c : 2 * K * (c + 1)], in_=s_flat[:, 2 * K * c : 2 * K * (c + 1)])
-
-        def load_b(w):
-            nc.sync.dma_start(
-                out=b_sb[w][:].rearrange("p (j t) -> p j t", t=NT), in_=b_dram[w].rearrange("j (p t) -> p j t", t=NT)
-            )
 
         def flip(key, src32, stride):
             tp = pst.tile([P, 512], F32, tag="tp")
@@ -106,29 +114,29 @@ def tile_skill_net_pa_kernel(tc, s, ei1, ej1, w11, b11, w12, b12, out):
         def t_s(c):
             flip(("s", c), s_sb[:].bitcast(F32)[:, 512 * c : 512 * c + 512], 2)
 
-        def eq_s(c):
-            g = work.tile([P, 1024], BF16, align_bytes=64, tag="gs", bufs=2)
-            regroup(vcopy, g[:].bitcast(F32), ("s", c))
+        def e_s(c):
+            grouped[("s", c)] = work.tile([P, 1024], BF16, align_bytes=64, tag="gs", name="gs")
+            regroup(vcopy, grouped[("s", c)][:].bitcast(F32), ("s", c))
+
+        def q_s(c):
             nc.vector.quantize_mx(
                 out=s_codes[:, 256 * c : 256 * c + 256].bitcast(FP8X4),
                 scales=s_scales[:, 256 * c : 256 * c + 256],
-                in_=g[:],
+                in_=grouped[("s", c)][:],
             )
 
         def t_f(hh):
-            flip(("f", hh), rep[:, 512 * hh : 512 * hh + 512], 1)
+            tp = pst.tile([P, 512], F32, tag="tp")
+            for a in range(4):
+                col = NJ + 4 * hh + a
+                nc.tensor.transpose(tp[:, P * a : P * a + P], f[:, col : col + 1].to_broadcast([P, P]), ident[:])
+            banks[("f", hh)] = tp
 
         def e_f(hh):
             vcopy(out=fi_all[:, 512 * hh : 512 * hh + 512], in_=banks[("f", hh)][:])
 
-        def open_bank(j, w):
-            acc[(w, j)] = psx.tile([P, 512], F32, tag="mx", name="mx")
-
-        def mx(j, w, n_dummy):
-            if (w, j) not in acc:
-                open_bank(j, w)
-            ps = acc[(w, j)]
-            for t in range(NT):
+        def mx_pass(ps, j, w, ts):
+            for t in ts:
                 nc.tensor.matmul_mx(
                     out=ps[:, P * t : P * t + P],
                     lhsT=codes[(w, j)][:, P * t : P * t + P].bitcast(FP8X4),
@@ -139,6 +147,10 @@ def tile_skill_net_pa_kernel(tc, s, ei1, ej1, w11, b11, w12, b12, out):
                     stop=True,
                 )
 
+        def mx(j, w):
+            acc[(w, j)] = psx.tile([P, 512], F32, tag="mx", name="mx")
+            mx_pass(acc[(w, j)], j, w, range(NT))
+
         def x_(j):
             e = work.tile([P, 512], F32, tag="e")
             for t in range(NT):
@@ -146,176 +158,236 @@ def tile_skill_net_pa_kernel(tc, s, ei1, ej1, w11, b11, w12, b12, out):
                     out=e[:, P * t : P * t + P],
                     in_=acc[(LS, j)][:, P * t : P * t + P],
                     func=ACT.Exp,
-                    bias=b_sb[LS][:, NT * j + t : NT * j + t + 1],
+                    bias=vec[:, NJ + NT * j + t : NJ + NT * j + t + 1],
                     scale=1.0,
                 )
             sb[("e", j)] = e
 
-        def czo(j):
-            a_sb = work.tile([P, 512], F32, tag="a")
-            nc.vector.tensor_scalar(
-                out=a_sb[:],
-                in0=sb[("e", j)][:],
-                scalar1=ebounds[:, 0:1],
-                scalar2=ebounds[:, 1:2],
-                op0=ALU.max,
-                op1=ALU.min,
-            )
-            z = work.tile([P, 512], F32, tag="z")
-            o = work.tile([P, 512], F32, tag="o")
+        def t_o(j):
+            ot = pso.tile([P, 512], F32, tag="ot")
             for t in range(NT):
-                nc.vector.scalar_tensor_tensor(
-                    out=z[:, P * t : P * t + P],
-                    in0=a_sb[:, P * t : P * t + P],
-                    scalar=f[:, NT * j + t : NT * j + t + 1],
-                    in1=fi_all[:, P * j : P * j + P],
-                    op0=ALU.mult,
-                    op1=ALU.mult,
-                )
-            for t in range(NT):
-                nc.vector.scalar_tensor_tensor(
-                    out=o[:, P * t : P * t + P],
-                    in0=acc[(MU, j)][:, P * t : P * t + P],
-                    scalar=b_sb[MU][:, NT * j + t : NT * j + t + 1],
-                    in1=z[:, P * t : P * t + P],
-                    op0=ALU.add,
-                    op1=ALU.add,
-                )
-            sb[("o", j)] = o
-
-        def ot_(j, ot, n_matmul):
-            for t in range(NT):
-                if t < n_matmul:
-                    nc.tensor.matmul(
-                        out=ot[:, P * t : P * t + P],
-                        lhsT=sb[("o", j)][:, P * t : P * t + P],
-                        rhs=ident[:],
-                        start=True,
-                        stop=True,
-                    )
-                else:
-                    nc.tensor.transpose(ot[:, P * t : P * t + P], sb[("o", j)][:, P * t : P * t + P], ident[:])
+                nc.tensor.transpose(ot[:, P * t : P * t + P], sb[("o", j)][:, P * t : P * t + P], ident[:])
             banks[("o", j)] = ot
 
         def r_(j):
             r = work.tile([P, 512], F32, tag="r", bufs=3)
             nc.scalar.activation(
-                out=r[:].rearrange("i (p t) -> i p t", t=NT),
-                in_=banks[("o", j)][:].rearrange("i (t p) -> i p t", t=NT),
+                out=r[:].rearrange("i (h p u) -> i h p u", h=2, u=2),
+                in_=banks[("o", j)][:].rearrange("i (h u p) -> i h p u", h=2, u=2),
                 func=ACT.Relu,
             )
             nc.sync.dma_start(out=out[:, j, :], in_=r[:])
 
-        nc.sync.dma_start(
-            out=noise_in[:, 0:NJ].rearrange("p (j t) -> p j t", t=NT),
-            in_=ej1.rearrange("o j (p t) -> p (o j) t", t=NT),
-        )
-        nc.sync.dma_start(out=noise_in[:, NJ : NJ + NM], in_=ei1.rearrange("i j o -> i (j o)"))
+        def q_half(h):
+            if h == 0:
+                codes[(MU, NM - 1)] = work.tile([P, 512], U32, align_bytes=64, tag="cw", bufs=4, name="cw")
+                scales[(MU, NM - 1)] = work.tile([P, 512], U8, align_bytes=64, tag="sw", bufs=4, name="sw")
+            cols = slice(256 * h, 256 * (h + 1))
+            nc.vector.quantize_mx(
+                out=codes[(MU, NM - 1)][:, cols].bitcast(FP8X4),
+                scales=scales[(MU, NM - 1)][:, cols],
+                in_=grouped[(MU, NM - 1)][:, 1024 * h : 1024 * (h + 1)],
+            )
+
+        def mx_half(h):
+            acc[(MU, NM - 1, h)] = psx.tile([P, 512], F32, tag="mx", name="mx")
+            mx_pass(acc[(MU, NM - 1, h)], NM - 1, MU, (2 * h, 2 * h + 1))
+
+        def o_half(h):
+            sb[("o", NM - 1, h)] = work.tile([P, 256], F32, tag="oh", name="oh")
+            o_pass(acc[(MU, NM - 1, h)], sb[("o", NM - 1, h)], 256 * h, NM - 1, (2 * h, 2 * h + 1))
+
+        def t_o_half(h):
+            ot = pst.tile([P, 512], F32, tag="tp")
+            for u in range(2):
+                nc.tensor.transpose(ot[:, P * u : P * u + P], sb[("o", NM - 1, h)][:, P * u : P * u + P], ident[:])
+            banks[("o", NM - 1, h)] = ot
+
+        def r_half(h):
+            r = work.tile([P, 256], F32, tag="rh", name="rh")
+            dst = r[:].rearrange("i (p u) -> i p u", u=2)
+            src = banks[("o", NM - 1, h)][:, 0:256].rearrange("i (u p) -> i p u", u=2)
+            if h == 0:
+                nc.scalar.activation(out=dst, in_=src, func=ACT.Relu)
+            else:
+                nc.vector.tensor_scalar_max(out=dst, in0=src, scalar1=0.0)
+            nc.sync.dma_start(out=out[:, NM - 1, 256 * h : 256 * (h + 1)], in_=r[:])
+
+        nc.gpsimd.memset(vec_rows[:].bitcast(U32), 0)
+        for v, dram in enumerate((ej1.rearrange("o j l -> (o j) l"), b12, b11)):
+            nc.scalar.dma_start(out=vec_rows[NM * v : NM * (v + 1), :], in_=dram)
+        nc.scalar.dma_start(out=ei_in[:], in_=ei1.rearrange("i j o -> i (j o)"))
+        load_w(0, LS, 2)
         load_s(0)
-        load_w(0)
-        load_w(1)
-        load_b(LS)
+        load_w(1, LS, 2)
+        load_w(0, MU, 2)
         load_s(1)
-        load_w(2)
-        load_b(MU)
-        load_s(2)
-        load_w(3)
-        load_s(3)
-        for j in range(4, NM):
-            load_w(j)
+        for j in range(2, NM):
+            load_w(j, LS, 1)
+            load_w(j - 1, MU, 1)
+            if j in (3, 5):
+                load_s(j // 2 + 1)
+        load_w(NM - 1, MU, 2)
 
-        with tc.manual_schedule():
-            make_identity(nc, ident[:])
-            nc.vector.memset(bounds[:, 0:1], -20.0)
-            nc.vector.memset(bounds[:, 1:2], 4.0)
-            nc.scalar.activation(out=warm[:], in_=bounds[:, 1:2], func=ACT.Sqrt)
+        def t_vec():
+            tv = pst.tile([P, NT * P], BF16, tag="tp")
+            for t in range(NT):
+                nc.tensor.transpose(tv[:, P * t : P * t + P], vec_rows[:, 256 * (t // 2) + t % 2 : 256 * (t // 2 + 1) : 2], ident16[:])
+            banks["vec"] = tv
 
+        def e_vec():
+            vcopy(
+                out=vec[:].rearrange("p (r t) -> p r t", t=NT),
+                in_=banks["vec"][:].rearrange("p (t r) -> p r t", t=NT)[:, 0 : 3 * NM, :],
+            )
+
+        def noise():
+            nc.gpsimd.tensor_copy(out=noise_in[:, 0:NJ], in_=vec[:, 0:NJ])
+            nc.gpsimd.tensor_copy(out=noise_in[:, NJ : NJ + NM], in_=ei_in[:])
             nc.vector.scalar_tensor_tensor(
                 out=mag[:], in0=noise_in[:], scalar=-1.0, in1=noise_in[:], op0=ALU.mult, op1=ALU.max
             )
-            nc.vector.tensor_scalar_max(out=mag[:], in0=mag[:], scalar1=2.0 ** -116)
-            nc.vector.tensor_single_scalar(out=neg[:], in_=noise_in[:], scalar=0.0, op=ALU.is_lt)
-            nc.vector.scalar_tensor_tensor(
-                out=sgn[:], in0=noise_in[:], scalar=0.0, in1=neg[:], op0=ALU.is_gt, op1=ALU.subtract
-            )
+            nc.gpsimd.tensor_scalar(out=neg[:], in0=noise_in[:], scalar1=0.0, scalar2=None, op0=ALU.is_lt)
+            nc.gpsimd.tensor_scalar(out=sgn[:], in0=noise_in[:], scalar1=0.0, scalar2=None, op0=ALU.is_gt)
+            nc.gpsimd.tensor_tensor(out=sgn[:], in0=sgn[:], in1=neg[:], op=ALU.subtract)
             nc.scalar.activation(out=root[:], in_=mag[:], func=ACT.Sqrt)
-            nc.scalar.activation(out=ebounds[:], in_=bounds[:], func=ACT.Exp)
-            nc.vector.tensor_mul(out=f[:], in0=root[:], in1=sgn[:])
-            nc.gpsimd.tensor_scalar(
-                out=rep[:].rearrange("i (j c) -> i j c", j=NM),
-                in0=f[:, NJ : NJ + NM].unsqueeze(2).to_broadcast([P, NM, P]),
-                scalar1=1.0,
-                scalar2=0.0,
-                op0=ALU.mult,
-                op1=ALU.add,
+            nc.scalar.activation(out=warm[:], in_=root[:, 0:1], func=ACT.Exp)
+            nc.gpsimd.tensor_tensor(out=f[:], in0=root[:], in1=sgn[:], op=ALU.mult)
+
+        def clip(j):
+            a_sb = work.tile([P, 512], F32, tag="a")
+            nc.vector.tensor_scalar(
+                out=a_sb[:],
+                in0=sb[("e", j)][:],
+                scalar1=math.exp(-20.0),
+                scalar2=math.exp(4.0),
+                op0=ALU.max,
+                op1=ALU.min,
             )
+            sb[("a", j)] = a_sb
 
-        t_s(0)
-        eq_s(0)
-        t_w(0, LS, 0)
-        t_w(0, LS, 1)
-        e_w(0, LS, 0, scopy)
-        e_w(0, LS, 1, vcopy)
-        t_w(0, MU, 0)
-        t_w(0, MU, 1)
-        q_w(0, LS)
-        e_w(0, MU, 0, scopy)
-        e_w(0, MU, 1, vcopy)
-        q_w(0, MU)
-        t_w(1, LS, 0)
-        t_w(1, LS, 1)
-        t_f(0)
-        e_f(0)
-        t_w(1, MU, 0)
+        def z_(j):
+            z = work.tile([P, 512], F32, tag="z")
+            for t in range(NT):
+                nc.vector.scalar_tensor_tensor(
+                    out=z[:, P * t : P * t + P],
+                    in0=sb[("a", j)][:, P * t : P * t + P],
+                    scalar=f[:, NT * j + t : NT * j + t + 1],
+                    in1=fi_all[:, P * j : P * j + P],
+                    op0=ALU.mult,
+                    op1=ALU.mult,
+                )
+            sb[("z", j)] = z
 
-        chores = {0: ("s", 1), 1: ("s", 2), 2: ("f", 1), 3: ("s", 3)}
-        for n in range(NM + 2):
-            j = n + 1
-            d = n - 1
-            chore = chores.get(n)
-            if n < NM:
-                mx(n, LS, 0)
-                mx(n, MU, 0)
-            if n == 0:
-                t_w(1, MU, 1)
-            if 0 <= d < NM:
-                czo(d)
-            if j < NM:
-                e_w(j, LS, 0, scopy)
-            if n >= 2:
-                r_(n - 2)
-            if chore:
-                if chore[0] == "s":
-                    t_s(chore[1])
-                else:
-                    t_f(chore[1])
-            if j < NM:
-                e_w(j, LS, 1, scopy)
-            if j + 1 < NM:
-                t_w(j + 1, LS, 0)
-            if chore:
-                if chore[0] == "s":
-                    eq_s(chore[1])
-                else:
-                    e_f(chore[1])
-            if j < NM:
-                q_w(j, LS)
-                e_w(j, MU, 0, scopy)
-            if j + 1 < NM:
-                t_w(j + 1, LS, 1)
-            if j < NM:
-                e_w(j, MU, 1, scopy)
-            if 0 <= d < NM:
-                if d == NM - 1:
-                    last_ot = pst.tile([P, 512], F32, tag="tp")
-                    ot_(d, last_ot, 0)
-                else:
-                    ot = pso.tile([P, 512], F32, tag="ot")
-                    ot_(d, ot, 0)
-            if j + 1 < NM:
-                t_w(j + 1, MU, 0)
-                t_w(j + 1, MU, 1)
-            if j < NM:
-                q_w(j, MU)
-            if n < NM:
-                x_(n)
+        def o_pass(ps, o, first, j, ts):
+            for t in ts:
+                nc.vector.scalar_tensor_tensor(
+                    out=o[:, P * t - first : P * t + P - first],
+                    in0=ps[:, P * t : P * t + P],
+                    scalar=vec[:, 2 * NJ + NT * j + t : 2 * NJ + NT * j + t + 1],
+                    in1=sb[("z", j)][:, P * t : P * t + P],
+                    op0=ALU.add,
+                    op1=ALU.add,
+                )
+
+        def o_(j):
+            sb[("o", j)] = work.tile([P, 512], F32, tag="o", name="o")
+            o_pass(acc[(MU, j)], sb[("o", j)], 0, j, range(NT))
+
+        with tc.manual_schedule():
+            make_identity(nc, ident[:])
+            nc.vector.memset(warm[:], 1.0)
+            nc.scalar.activation(out=warm[:], in_=warm[:], func=ACT.Sqrt)
+            vcopy(out=ident16[:], in_=ident[:])
+            t_vec()
+            t_w(0, LS, 0)
+            e_vec()
+            noise()
+            e_w(0, LS, 0, vcopy)
+            t_w(0, LS, 1)
+            e_w(0, LS, 1, vcopy)
+            t_s(0)
+            e_s(0)
+            t_w(1, LS, 0)
+            t_w(1, LS, 1)
+            q_w(0, LS)
+            q_s(0)
+            t_w(0, MU, 0)
+            t_w(0, MU, 1)
+            s_at = {0: 1, 2: 2, 4: 3}
+            f_at = {1: 0, 3: 1}
+            for n in range(NM - 1):
+                if n == 0:
+                    mx(0, LS)
+                if n + 1 < NM:
+                    e_w(n + 1, LS, 0, scopy)
+                if 0 <= n - 1 < NM:
+                    clip(n - 1)
+                if n - 1 in s_at:
+                    q_s(s_at[n - 1])
+                if n + 2 < NM:
+                    t_w(n + 2, LS, 0)
+                if n >= 2:
+                    t_o(n - 2)
+                if n in f_at:
+                    t_f(f_at[n])
+                if n in f_at:
+                    e_f(f_at[n])
+                if 0 <= n - 1 < NM:
+                    z_(n - 1)
+                if n + 1 < NM:
+                    e_w(n + 1, LS, 1, scopy)
+                if n + 2 < NM:
+                    t_w(n + 2, LS, 1)
+                if n == 0:
+                    x_(0)
+                if 0 < n < NM:
+                    mx(n, LS)
+                if 0 <= n - 1 < NM:
+                    mx(n - 1, MU)
+                if n + 1 < NM:
+                    q_w(n + 1, LS)
+                if n in s_at:
+                    t_s(s_at[n])
+                if n in s_at:
+                    e_s(s_at[n])
+                if n < NM:
+                    e_w(n, MU, 0, scopy)
+                if n + 1 < NM:
+                    t_w(n + 1, MU, 0)
+                if 0 <= n - 1 < NM:
+                    o_(n - 1)
+                if n >= 2:
+                    r_(n - 2)
+                if n < NM:
+                    e_w(n, MU, 1, scopy)
+                if n < NM:
+                    q_w(n, MU)
+                if n + 1 < NM:
+                    t_w(n + 1, MU, 1)
+                if 0 < n < NM:
+                    x_(n)
+            clip(NM - 2)
+            e_w(NM - 1, MU, 0, scopy)
+            mx(NM - 1, LS)
+            mx(NM - 2, MU)
+            t_o(NM - 3)
+            z_(NM - 2)
+            q_half(0)
+            e_w(NM - 1, MU, 1, scopy)
+            x_(NM - 1)
+            q_half(1)
+            mx_half(0)
+            mx_half(1)
+            o_(NM - 2)
+            t_o(NM - 2)
+            r_(NM - 3)
+            clip(NM - 1)
+            z_(NM - 1)
+            r_(NM - 2)
+            o_half(0)
+            t_o_half(0)
+            o_half(1)
+            t_o_half(1)
+            r_half(0)
+            r_half(1)

@@ -25,9 +25,9 @@ def tile_skill_net_pa_kernel(tc, s, ei1, ej1, w11, b11, w12, b12, out):
     nc = tc.nc
     with tc.tile_pool(name="const", bufs=1) as const, tc.tile_pool(name="raw", bufs=1) as raw, tc.tile_pool(
         name="work", bufs=2
-    ) as work, tc.psum_pool(name="pst", bufs=4) as pst, tc.psum_pool(name="psx", bufs=3) as psx, tc.psum_pool(
+    ) as work, tc.psum_pool(name="pst", bufs=4) as pst, tc.psum_pool(name="psx", bufs=2) as psx, tc.psum_pool(
         name="pso", bufs=1
-    ) as pso:
+    ) as pso, tc.psum_pool(name="psf", bufs=1) as psf:
         vcopy = nc.vector.tensor_copy
         scopy = nc.scalar.copy
 
@@ -46,7 +46,6 @@ def tile_skill_net_pa_kernel(tc, s, ei1, ej1, w11, b11, w12, b12, out):
         sgn = const.tile([P, NJ + NM], F32)
         root = const.tile([P, NJ + NM], F32)
         f = const.tile([P, NJ + NM], F32)
-        fi_all = const.tile([P, NM * P], F32)
         s_codes = const.tile([P, NM * P], U32, align_bytes=64)
         s_scales = const.tile([P, NM * P], U8, align_bytes=64)
         s_sb = raw.tile([P, NM * K], BF16)
@@ -65,17 +64,10 @@ def tile_skill_net_pa_kernel(tc, s, ei1, ej1, w11, b11, w12, b12, out):
 
         def load_w(j, w, parts):
             width = NT * K // parts
-            if parts == 1:
-                nc.sync.dma_start(
-                    out=w_sb[(w, j)][:].rearrange("p (h c) -> p h c", h=2),
-                    in_=w_dram[w][j].rearrange("(h p u) k -> p h (u k)", h=2, u=2),
-                )
-            else:
-                for h in range(2):
-                    nc.sync.dma_start(
-                        out=w_sb[(w, j)][:, width * h : width * (h + 1)],
-                        in_=w_dram[w][j][256 * h : 256 * (h + 1), :].rearrange("(p u) k -> p (u k)", u=2),
-                    )
+            flat = w_dram[w][j].rearrange("(p t) k -> p (t k)", t=NT)
+            for c in range(parts):
+                cols = slice(width * c, width * (c + 1))
+                nc.sync.dma_start(out=w_sb[(w, j)][:, cols], in_=flat[:, cols])
 
         def load_s(c):
             s_flat = s.rearrange("i j k -> i (j k)")
@@ -104,11 +96,14 @@ def tile_skill_net_pa_kernel(tc, s, ei1, ej1, w11, b11, w12, b12, out):
                 grouped[(w, j)] = work.tile([P, 2048], BF16, align_bytes=64, tag="g", bufs=4, name="g")
             regroup(copy, grouped[(w, j)][:].bitcast(F32)[:, 512 * h : 512 * h + 512], (w, j, h))
 
-        def q_w(j, w):
-            codes[(w, j)] = work.tile([P, 512], U32, align_bytes=64, tag="cw", bufs=4, name="cw")
-            scales[(w, j)] = work.tile([P, 512], U8, align_bytes=64, tag="sw", bufs=4, name="sw")
+        def q_w(j, w, first=0, last=512):
+            if first == 0:
+                codes[(w, j)] = work.tile([P, 512], U32, align_bytes=64, tag="cw", bufs=4, name="cw")
+                scales[(w, j)] = work.tile([P, 512], U8, align_bytes=64, tag="sw", bufs=4, name="sw")
             nc.vector.quantize_mx(
-                out=codes[(w, j)][:].bitcast(FP8X4), scales=scales[(w, j)][:], in_=grouped[(w, j)][:]
+                out=codes[(w, j)][:, first:last].bitcast(FP8X4),
+                scales=scales[(w, j)][:, first:last],
+                in_=grouped[(w, j)][:, 4 * first : 4 * last],
             )
 
         def t_s(c):
@@ -126,14 +121,11 @@ def tile_skill_net_pa_kernel(tc, s, ei1, ej1, w11, b11, w12, b12, out):
             )
 
         def t_f(hh):
-            tp = pst.tile([P, 512], F32, tag="tp")
+            fi = psf.tile([P, 512], F32, tag="fi")
             for a in range(4):
                 col = NJ + 4 * hh + a
-                nc.tensor.transpose(tp[:, P * a : P * a + P], f[:, col : col + 1].to_broadcast([P, P]), ident[:])
-            banks[("f", hh)] = tp
-
-        def e_f(hh):
-            vcopy(out=fi_all[:, 512 * hh : 512 * hh + 512], in_=banks[("f", hh)][:])
+                nc.tensor.transpose(fi[:, P * a : P * a + P], f[:, col : col + 1].to_broadcast([P, P]), ident[:])
+            banks[("f", hh)] = fi
 
         def mx_pass(ps, j, w, ts):
             for t in ts:
@@ -172,22 +164,11 @@ def tile_skill_net_pa_kernel(tc, s, ei1, ej1, w11, b11, w12, b12, out):
         def r_(j):
             r = work.tile([P, 512], F32, tag="r", bufs=3)
             nc.scalar.activation(
-                out=r[:].rearrange("i (h p u) -> i h p u", h=2, u=2),
-                in_=banks[("o", j)][:].rearrange("i (h u p) -> i h p u", h=2, u=2),
+                out=r[:].rearrange("i (p t) -> i p t", t=NT),
+                in_=banks[("o", j)][:].rearrange("i (t p) -> i p t", t=NT),
                 func=ACT.Relu,
             )
             nc.sync.dma_start(out=out[:, j, :], in_=r[:])
-
-        def q_half(h):
-            if h == 0:
-                codes[(MU, NM - 1)] = work.tile([P, 512], U32, align_bytes=64, tag="cw", bufs=4, name="cw")
-                scales[(MU, NM - 1)] = work.tile([P, 512], U8, align_bytes=64, tag="sw", bufs=4, name="sw")
-            cols = slice(256 * h, 256 * (h + 1))
-            nc.vector.quantize_mx(
-                out=codes[(MU, NM - 1)][:, cols].bitcast(FP8X4),
-                scales=scales[(MU, NM - 1)][:, cols],
-                in_=grouped[(MU, NM - 1)][:, 1024 * h : 1024 * (h + 1)],
-            )
 
         def mx_half(h):
             acc[(MU, NM - 1, h)] = psx.tile([P, 512], F32, tag="mx", name="mx")
@@ -204,19 +185,20 @@ def tile_skill_net_pa_kernel(tc, s, ei1, ej1, w11, b11, w12, b12, out):
             banks[("o", NM - 1, h)] = ot
 
         def r_half(h):
-            r = work.tile([P, 256], F32, tag="rh", name="rh")
-            dst = r[:].rearrange("i (p u) -> i p u", u=2)
+            if h == 0:
+                sb["r"] = work.tile([P, 512], F32, tag="r", bufs=3, name="r")
+            dst = sb["r"][:].rearrange("i (p h u) -> i h p u", h=2, u=2)[:, h]
             src = banks[("o", NM - 1, h)][:, 0:256].rearrange("i (u p) -> i p u", u=2)
             if h == 0:
                 nc.scalar.activation(out=dst, in_=src, func=ACT.Relu)
             else:
                 nc.vector.tensor_scalar_max(out=dst, in0=src, scalar1=0.0)
-            nc.sync.dma_start(out=out[:, NM - 1, 256 * h : 256 * (h + 1)], in_=r[:])
+                nc.sync.dma_start(out=out[:, NM - 1, :], in_=sb["r"][:])
 
         nc.gpsimd.memset(vec_rows[:].bitcast(U32), 0)
         for v, dram in enumerate((ej1.rearrange("o j l -> (o j) l"), b12, b11)):
-            nc.scalar.dma_start(out=vec_rows[NM * v : NM * (v + 1), :], in_=dram)
-        nc.scalar.dma_start(out=ei_in[:], in_=ei1.rearrange("i j o -> i (j o)"))
+            nc.sync.dma_start(out=vec_rows[NM * v : NM * (v + 1), :], in_=dram)
+        nc.sync.dma_start(out=ei_in[:], in_=ei1.rearrange("i j o -> i (j o)"))
         load_w(0, LS, 2)
         load_s(0)
         load_w(1, LS, 2)
@@ -232,7 +214,7 @@ def tile_skill_net_pa_kernel(tc, s, ei1, ej1, w11, b11, w12, b12, out):
         def t_vec():
             tv = pst.tile([P, NT * P], BF16, tag="tp")
             for t in range(NT):
-                nc.tensor.transpose(tv[:, P * t : P * t + P], vec_rows[:, 256 * (t // 2) + t % 2 : 256 * (t // 2 + 1) : 2], ident16[:])
+                nc.tensor.transpose(tv[:, P * t : P * t + P], vec_rows[:, t::NT], ident16[:])
             banks["vec"] = tv
 
         def e_vec():
@@ -273,7 +255,7 @@ def tile_skill_net_pa_kernel(tc, s, ei1, ej1, w11, b11, w12, b12, out):
                     out=z[:, P * t : P * t + P],
                     in0=sb[("a", j)][:, P * t : P * t + P],
                     scalar=f[:, NT * j + t : NT * j + t + 1],
-                    in1=fi_all[:, P * j : P * j + P],
+                    in1=banks[("f", j // 4)][:, P * (j % 4) : P * (j % 4) + P],
                     op0=ALU.mult,
                     op1=ALU.mult,
                 )
@@ -294,100 +276,97 @@ def tile_skill_net_pa_kernel(tc, s, ei1, ej1, w11, b11, w12, b12, out):
             sb[("o", j)] = work.tile([P, 512], F32, tag="o", name="o")
             o_pass(acc[(MU, j)], sb[("o", j)], 0, j, range(NT))
 
-        with tc.manual_schedule():
-            make_identity(nc, ident[:])
-            nc.vector.memset(warm[:], 1.0)
-            nc.scalar.activation(out=warm[:], in_=warm[:], func=ACT.Sqrt)
-            vcopy(out=ident16[:], in_=ident[:])
-            t_vec()
-            t_w(0, LS, 0)
-            e_vec()
-            noise()
-            e_w(0, LS, 0, vcopy)
-            t_w(0, LS, 1)
-            e_w(0, LS, 1, vcopy)
-            t_s(0)
-            e_s(0)
-            t_w(1, LS, 0)
-            t_w(1, LS, 1)
-            q_w(0, LS)
-            q_s(0)
-            t_w(0, MU, 0)
-            t_w(0, MU, 1)
-            s_at = {0: 1, 2: 2, 4: 3}
-            f_at = {1: 0, 3: 1}
-            for n in range(NM - 1):
-                if n == 0:
-                    mx(0, LS)
-                if n + 1 < NM:
-                    e_w(n + 1, LS, 0, scopy)
-                if 0 <= n - 1 < NM:
-                    clip(n - 1)
-                if n - 1 in s_at:
-                    q_s(s_at[n - 1])
-                if n + 2 < NM:
-                    t_w(n + 2, LS, 0)
-                if n >= 2:
-                    t_o(n - 2)
-                if n in f_at:
-                    t_f(f_at[n])
-                if n in f_at:
-                    e_f(f_at[n])
-                if 0 <= n - 1 < NM:
-                    z_(n - 1)
-                if n + 1 < NM:
-                    e_w(n + 1, LS, 1, scopy)
-                if n + 2 < NM:
-                    t_w(n + 2, LS, 1)
-                if n == 0:
-                    x_(0)
-                if 0 < n < NM:
-                    mx(n, LS)
-                if 0 <= n - 1 < NM:
-                    mx(n - 1, MU)
-                if n + 1 < NM:
-                    q_w(n + 1, LS)
-                if n in s_at:
-                    t_s(s_at[n])
-                if n in s_at:
-                    e_s(s_at[n])
-                if n < NM:
-                    e_w(n, MU, 0, scopy)
-                if n + 1 < NM:
-                    t_w(n + 1, MU, 0)
-                if 0 <= n - 1 < NM:
-                    o_(n - 1)
-                if n >= 2:
-                    r_(n - 2)
-                if n < NM:
-                    e_w(n, MU, 1, scopy)
-                if n < NM:
-                    q_w(n, MU)
-                if n + 1 < NM:
-                    t_w(n + 1, MU, 1)
-                if 0 < n < NM:
-                    x_(n)
-            clip(NM - 2)
-            e_w(NM - 1, MU, 0, scopy)
-            mx(NM - 1, LS)
-            mx(NM - 2, MU)
-            t_o(NM - 3)
-            z_(NM - 2)
-            q_half(0)
-            e_w(NM - 1, MU, 1, scopy)
-            x_(NM - 1)
-            q_half(1)
-            mx_half(0)
-            mx_half(1)
-            o_(NM - 2)
-            t_o(NM - 2)
-            r_(NM - 3)
-            clip(NM - 1)
-            z_(NM - 1)
-            r_(NM - 2)
-            o_half(0)
-            t_o_half(0)
-            o_half(1)
-            t_o_half(1)
-            r_half(0)
-            r_half(1)
+        make_identity(nc, ident[:])
+        nc.vector.memset(warm[:], 1.0)
+        nc.scalar.activation(out=warm[:], in_=warm[:], func=ACT.Sqrt)
+        vcopy(out=ident16[:], in_=ident[:])
+        t_vec()
+        t_w(0, LS, 0)
+        e_vec()
+        noise()
+        e_w(0, LS, 0, vcopy)
+        t_w(0, LS, 1)
+        e_w(0, LS, 1, vcopy)
+        t_s(0)
+        e_s(0)
+        t_w(1, LS, 0)
+        t_w(1, LS, 1)
+        q_w(0, LS)
+        q_s(0)
+        t_w(0, MU, 0)
+        t_w(0, MU, 1)
+        s_at = {0: 1, 2: 2, 4: 3}
+        f_at = {0: 0, 4: 1}
+        for n in range(NM - 1):
+            if n == 0:
+                mx(0, LS)
+            if n + 1 < NM:
+                e_w(n + 1, LS, 0, scopy)
+            if 0 <= n - 1 < NM:
+                clip(n - 1)
+            if n - 1 in s_at:
+                q_s(s_at[n - 1])
+            if n + 2 < NM:
+                t_w(n + 2, LS, 0)
+            if n >= 2:
+                t_o(n - 2)
+            if 0 <= n - 1 < NM:
+                z_(n - 1)
+            if n + 1 < NM:
+                e_w(n + 1, LS, 1, scopy)
+            if n + 2 < NM:
+                t_w(n + 2, LS, 1)
+            if n == 0:
+                x_(0)
+            if 0 < n < NM:
+                mx(n, LS)
+            if 0 <= n - 1 < NM:
+                mx(n - 1, MU)
+            if n in f_at:
+                t_f(f_at[n])
+            if n + 1 < NM:
+                q_w(n + 1, LS)
+            if n in s_at:
+                t_s(s_at[n])
+            if n in s_at:
+                e_s(s_at[n])
+            if n < NM:
+                e_w(n, MU, 0, scopy)
+            if n + 1 < NM:
+                t_w(n + 1, MU, 0)
+            if 0 <= n - 1 < NM:
+                o_(n - 1)
+            if n >= 2:
+                r_(n - 2)
+            if n < NM:
+                e_w(n, MU, 1, scopy)
+            if n < NM:
+                q_w(n, MU)
+            if n + 1 < NM:
+                t_w(n + 1, MU, 1)
+            if 0 < n < NM:
+                x_(n)
+        clip(NM - 2)
+        e_w(NM - 1, MU, 0, scopy)
+        mx(NM - 1, LS)
+        mx(NM - 2, MU)
+        t_o(NM - 3)
+        z_(NM - 2)
+        q_w(NM - 1, MU, 0, 256)
+        e_w(NM - 1, MU, 1, scopy)
+        x_(NM - 1)
+        q_w(NM - 1, MU, 256, 512)
+        mx_half(0)
+        mx_half(1)
+        o_(NM - 2)
+        t_o(NM - 2)
+        r_(NM - 3)
+        clip(NM - 1)
+        z_(NM - 1)
+        r_(NM - 2)
+        o_half(0)
+        t_o_half(0)
+        o_half(1)
+        t_o_half(1)
+        r_half(0)
+        r_half(1)

@@ -158,7 +158,11 @@ def tile_skill_net_pa_kernel(tc, s, ei1, ej1, w11, b11, w12, b12, out):
         def t_o(j):
             ot = pso.tile([P, 512], F32, tag="ot")
             for t in range(NT):
-                nc.tensor.transpose(ot[:, P * t : P * t + P], sb[("o", j)][:, P * t : P * t + P], ident[:])
+                o_t = sb[("o", j)][:, P * t : P * t + P]
+                if t < 2:
+                    nc.tensor.matmul(out=ot[:, P * t : P * t + P], lhsT=o_t, rhs=ident[:], start=True, stop=True)
+                else:
+                    nc.tensor.transpose(ot[:, P * t : P * t + P], o_t, ident[:])
             banks[("o", j)] = ot
 
         def r_(j):

@@ -159,7 +159,7 @@ def tile_skill_net_pa_kernel(tc, s, ei1, ej1, w11, b11, w12, b12, out):
             ot = pso.tile([P, 512], F32, tag="ot")
             for t in range(NT):
                 o_t = sb[("o", j)][:, P * t : P * t + P]
-                if t < 2:
+                if t < 1:
                     nc.tensor.matmul(out=ot[:, P * t : P * t + P], lhsT=o_t, rhs=ident[:], start=True, stop=True)
                 else:
                     nc.tensor.transpose(ot[:, P * t : P * t + P], o_t, ident[:])

@@ -24,10 +24,9 @@ LS, MU = 1, 0
 def tile_skill_net_pa_kernel(tc, s, ei1, ej1, w11, b11, w12, b12, out):
     nc = tc.nc
     with tc.tile_pool(name="const", bufs=1) as const, tc.tile_pool(name="raw", bufs=1) as raw, tc.tile_pool(
-        name="work", bufs=2
-    ) as work, tc.psum_pool(name="pst", bufs=4) as pst, tc.psum_pool(name="psx", bufs=2) as psx, tc.psum_pool(
-        name="pso", bufs=1
-    ) as pso, tc.psum_pool(name="psf", bufs=1) as psf:
+        name="work", bufs=3
+    ) as work, tc.psum_pool(name="pst", bufs=5) as pst, tc.psum_pool(name="psx", bufs=2) as psx, tc.psum_pool(
+        name="psf", bufs=1) as psf:
         vcopy = nc.vector.tensor_copy
         scopy = nc.scalar.copy
 
@@ -93,13 +92,13 @@ def tile_skill_net_pa_kernel(tc, s, ei1, ej1, w11, b11, w12, b12, out):
 
         def e_w(j, w, h, copy):
             if h == 0:
-                grouped[(w, j)] = work.tile([P, 2048], BF16, align_bytes=64, tag="g", bufs=4, name="g")
+                grouped[(w, j)] = work.tile([P, 2048], BF16, align_bytes=64, tag="g", bufs=6, name="g")
             regroup(copy, grouped[(w, j)][:].bitcast(F32)[:, 512 * h : 512 * h + 512], (w, j, h))
 
         def q_w(j, w, first=0, last=512):
             if first == 0:
-                codes[(w, j)] = work.tile([P, 512], U32, align_bytes=64, tag="cw", bufs=4, name="cw")
-                scales[(w, j)] = work.tile([P, 512], U8, align_bytes=64, tag="sw", bufs=4, name="sw")
+                codes[(w, j)] = work.tile([P, 512], U32, align_bytes=64, tag="cw", bufs=6, name="cw")
+                scales[(w, j)] = work.tile([P, 512], U8, align_bytes=64, tag="sw", bufs=6, name="sw")
             nc.vector.quantize_mx(
                 out=codes[(w, j)][:, first:last].bitcast(FP8X4),
                 scales=scales[(w, j)][:, first:last],
@@ -111,7 +110,7 @@ def tile_skill_net_pa_kernel(tc, s, ei1, ej1, w11, b11, w12, b12, out):
 
         def e_s(c):
             grouped[("s", c)] = work.tile([P, 1024], BF16, align_bytes=64, tag="gs", name="gs")
-            regroup(vcopy, grouped[("s", c)][:].bitcast(F32), ("s", c))
+            regroup(vcopy if c == 0 else scopy, grouped[("s", c)][:].bitcast(F32), ("s", c))
 
         def q_s(c):
             nc.vector.quantize_mx(
@@ -156,7 +155,7 @@ def tile_skill_net_pa_kernel(tc, s, ei1, ej1, w11, b11, w12, b12, out):
             sb[("e", j)] = e
 
         def t_o(j):
-            ot = pso.tile([P, 512], F32, tag="ot")
+            ot = pst.tile([P, 512], F32, tag="tp")
             for t in range(NT):
                 o_t = sb[("o", j)][:, P * t : P * t + P]
                 if t < 1:

@@ -206,8 +206,10 @@ def tile_skill_net_pa_kernel(tc, s, ei1, ej1, w11, b11, w12, b12, out):
         load_s(0)
         load_w(1, LS, 2)
         load_w(0, MU, 2)
+        load_w(2, LS, 2)
         load_s(1)
-        for j in range(2, NM):
+        load_w(1, MU, 2)
+        for j in range(3, NM):
             load_w(j, LS, 1)
             load_w(j - 1, MU, 1)
             if j in (3, 5):
@@ -311,8 +313,6 @@ def tile_skill_net_pa_kernel(tc, s, ei1, ej1, w11, b11, w12, b12, out):
                 q_s(s_at[n - 1])
             if n + 2 < NM:
                 t_w(n + 2, LS, 0)
-            if n >= 2:
-                t_o(n - 2)
             if 0 <= n - 1 < NM:
                 z_(n - 1)
             if n + 1 < NM:
@@ -337,10 +337,10 @@ def tile_skill_net_pa_kernel(tc, s, ei1, ej1, w11, b11, w12, b12, out):
                 e_w(n, MU, 0, scopy)
             if n + 1 < NM:
                 t_w(n + 1, MU, 0)
+            if n >= 2:
+                t_o(n - 2)
             if 0 <= n - 1 < NM:
                 o_(n - 1)
-            if n >= 2:
-                r_(n - 2)
             if n < NM:
                 e_w(n, MU, 1, scopy)
             if n < NM:
@@ -349,6 +349,8 @@ def tile_skill_net_pa_kernel(tc, s, ei1, ej1, w11, b11, w12, b12, out):
                 t_w(n + 1, MU, 1)
             if 0 < n < NM:
                 x_(n)
+            if n >= 2:
+                r_(n - 2)
         clip(NM - 2)
         e_w(NM - 1, MU, 0, scopy)
         mx(NM - 1, LS)

import math

import concourse.mybir as mybir
from concourse.masks import make_identity

F32 = mybir.dt.float32
BF16 = mybir.dt.bfloat16
U32 = mybir.dt.uint32
U8 = mybir.dt.uint8
I32 = mybir.dt.int32
FP8X4 = mybir.dt.float8_e4m3fn_x4
ALU = mybir.AluOpType
ACT = mybir.ActivationFunctionType

P = 128
NM = 8
K = 512
H = 512
NT = H // P
FLOPS = 2 * 2 * P * NM * K * H
LS, MU = 1, 0


def tile_skill_net_pa_kernel(tc, s, ei1, ej1, w11, b11, w12, b12, out):
    nc = tc.nc
    with tc.tile_pool(name="const", bufs=1) as const, tc.tile_pool(name="raw", bufs=1) as raw, tc.tile_pool(
        name="work", bufs=3
    ) as work, tc.psum_pool(name="pst", bufs=5) as pst, tc.psum_pool(name="psx", bufs=2) as psx, tc.psum_pool(
        name="psf", bufs=1) as psf:
        vcopy = nc.vector.tensor_copy
        scopy = nc.scalar.copy

        NJ = NM * NT
        vec_rows = const.tile([P, H], BF16)
        ei_in = const.tile([P, NM], BF16)
        vec = const.tile([P, 3 * NJ], F32)
        noise_in = const.tile([P, NJ + NM], F32)
        warm = const.tile([P, 1], F32)
        ident = const.tile([P, P], F32)
        ident16 = const.tile([P, P], BF16)
        iy = const.tile([P, NJ + NM], I32)
        xyy = const.tile([P, NJ + NM], F32)
        mag = const.tile([P, NJ + NM], F32)
        neg = const.tile([P, NJ + NM], F32)
        sgn = const.tile([P, NJ + NM], F32)
        root = const.tile([P, NJ + NM], F32)
        f = const.tile([P, NJ + NM], F32)
        s_codes = const.tile([P, NM * P], U32, align_bytes=64)
        s_scales = const.tile([P, NM * P], U8, align_bytes=64)
        s_sb = raw.tile([P, NM * K], BF16)
        w_dram = {LS: w12, MU: w11}
        w_sb = {}
        for j in range(NM):
            for w in (LS, MU):
                w_sb[(w, j)] = raw.tile([P, NT * K], BF16, name="w%d_%d" % (w, j))

        banks = {}
        grouped = {}
        codes = {}
        scales = {}
        acc = {}
        sb = {}

        def load_w(j, w, parts):
            width = NT * K // parts
            flat = w_dram[w][j].rearrange("(p t) k -> p (t k)", t=NT)
            for c in range(parts):
                cols = slice(width * c, width * (c + 1))
                nc.sync.dma_start(out=w_sb[(w, j)][:, cols], in_=flat[:, cols])

        def load_s(c):
            s_flat = s.rearrange("i j k -> i (j k)")
            nc.sync.dma_start(out=s_sb[:, 2 * K * c : 2 * K * (c + 1)], in_=s_flat[:, 2 * K * c : 2 * K * (c + 1)])

        def flip(key, src32, stride):
            tp = pst.tile([P, 512], F32, tag="tp")
            for a in range(4):
                first = P * stride * (a // stride) + a % stride
                nc.tensor.transpose(
                    tp[:, P * a : P * a + P], src32[:, first : P * stride * (a // stride + 1) : stride], ident[:]
                )
            banks[key] = tp

        def regroup(copy, dst32, key):
            copy(
                out=dst32.rearrange("q (a p u) -> q a p u", a=2, u=2),
                in_=banks[key][:].rearrange("q (a u p) -> q a p u", a=2, u=2),
            )

        def t_w(j, w, h):
            flip((w, j, h), w_sb[(w, j)][:].bitcast(F32)[:, 512 * h : 512 * h + 512], 2)

        def e_w(j, w, h, copy):
            if h == 0:
                grouped[(w, j)] = work.tile([P, 2048], BF16, align_bytes=64, tag="g", bufs=6, name="g")
            regroup(copy, grouped[(w, j)][:].bitcast(F32)[:, 512 * h : 512 * h + 512], (w, j, h))

        def q_w(j, w, first=0, last=512):
            if first == 0:
                codes[(w, j)] = work.tile([P, 512], U32, align_bytes=64, tag="cw", bufs=6, name="cw")
                scales[(w, j)] = work.tile([P, 512], U8, align_bytes=64, tag="sw", bufs=6, name="sw")
            nc.vector.quantize_mx(
                out=codes[(w, j)][:, first:last].bitcast(FP8X4),
                scales=scales[(w, j)][:, first:last],
                in_=grouped[(w, j)][:, 4 * first : 4 * last],
            )

        def t_s(c):
            flip(("s", c), s_sb[:].bitcast(F32)[:, 512 * c : 512 * c + 512], 2)

        def e_s(c):
            grouped[("s", c)] = work.tile([P, 1024], BF16, align_bytes=64, tag="gs", name="gs")
            regroup(vcopy if c == 0 else scopy, grouped[("s", c)][:].bitcast(F32), ("s", c))

        def q_s(c):
            nc.vector.quantize_mx(
                out=s_codes[:, 256 * c : 256 * c + 256].bitcast(FP8X4),
                scales=s_scales[:, 256 * c : 256 * c + 256],
                in_=grouped[("s", c)][:],
            )

        def t_f(hh):
            fi = psf.tile([P, 512], F32, tag="fi")
            for a in range(4):
                col = NJ + 4 * hh + a
                nc.tensor.transpose(fi[:, P * a : P * a + P], f[:, col : col + 1].to_broadcast([P, P]), ident[:])
            banks[("f", hh)] = fi

        def mx_pass(ps, j, w, ts):
            for t in ts:
                nc.tensor.matmul_mx(
                    out=ps[:, P * t : P * t + P],
                    lhsT=codes[(w, j)][:, P * t : P * t + P].bitcast(FP8X4),
                    lhsT_scale=scales[(w, j)][:, P * t : P * t + P],
                    rhs=s_codes[:, P * j : P * j + P].bitcast(FP8X4),
                    rhs_scale=s_scales[:, P * j : P * j + P],
                    start=True,
                    stop=True,
                )

        def mx(j, w):
            acc[(w, j)] = psx.tile([P, 512], F32, tag="mx", name="mx")
            mx_pass(acc[(w, j)], j, w, range(NT))

        def x_(j):
            e = work.tile([P, 512], F32, tag="e")
            for t in range(NT):
                nc.scalar.activation(
                    out=e[:, P * t : P * t + P],
                    in_=acc[(LS, j)][:, P * t : P * t + P],
                    func=ACT.Exp,
                    bias=vec[:, NJ + NT * j + t : NJ + NT * j + t + 1],
                    scale=1.0,
                )
            sb[("e", j)] = e

        def t_o(j):
            ot = pst.tile([P, 512], F32, tag="tp")
            for t in range(NT):
                o_t = sb[("o", j)][:, P * t : P * t + P]
                if t < 1:
                    nc.tensor.matmul(out=ot[:, P * t : P * t + P], lhsT=o_t, rhs=ident[:], start=True, stop=True)
                else:
                    nc.tensor.transpose(ot[:, P * t : P * t + P], o_t, ident[:])
            banks[("o", j)] = ot

        def r_(j):
            r = work.tile([P, 512], F32, tag="r", bufs=3)
            nc.scalar.activation(
                out=r[:].rearrange("i (p t) -> i p t", t=NT),
                in_=banks[("o", j)][:].rearrange("i (t p) -> i p t", t=NT),
                func=ACT.Relu,
            )
            nc.sync.dma_start(out=out[:, j, :], in_=r[:])

        def mx_half(h):
            acc[(MU, NM - 1, h)] = psx.tile([P, 512], F32, tag="mx", name="mx")
            mx_pass(acc[(MU, NM - 1, h)], NM - 1, MU, (2 * h, 2 * h + 1))

        def o_half(h):
            sb[("o", NM - 1, h)] = work.tile([P, 256], F32, tag="oh", name="oh")
            o_pass(acc[(MU, NM - 1, h)], sb[("o", NM - 1, h)], 256 * h, NM - 1, (2 * h, 2 * h + 1))

        def t_o_half(h):
            ot = pst.tile([P, 512], F32, tag="tp")
            for u in range(2):
                nc.tensor.transpose(ot[:, P * u : P * u + P], sb[("o", NM - 1, h)][:, P * u : P * u + P], ident[:])
            banks[("o", NM - 1, h)] = ot

        def r_half(h):
            if h == 0:
                sb["r"] = work.tile([P, 512], F32, tag="r", bufs=3, name="r")
            dst = sb["r"][:].rearrange("i (p h u) -> i h p u", h=2, u=2)[:, h]
            src = banks[("o", NM - 1, h)][:, 0:256].rearrange("i (u p) -> i p u", u=2)
            if h == 0:
                nc.scalar.activation(out=dst, in_=src, func=ACT.Relu)
            else:
                nc.vector.tensor_scalar_max(out=dst, in0=src, scalar1=0.0)
                nc.sync.dma_start(out=out[:, NM - 1, :], in_=sb["r"][:])

        nc.gpsimd.memset(vec_rows[:].bitcast(U32), 0)
        for v, dram in enumerate((ej1.rearrange("o j l -> (o j) l"), b12, b11)):
            nc.sync.dma_start(out=vec_rows[NM * v : NM * (v + 1), :], in_=dram)
        nc.sync.dma_start(out=ei_in[:], in_=ei1.rearrange("i j o -> i (j o)"))
        load_w(0, LS, 2)
        load_s(0)
        load_w(1, LS, 2)
        load_w(0, MU, 2)
        load_w(2, LS, 2)
        load_s(1)
        load_w(1, MU, 2)
        for j in range(3, NM):
            load_w(j, LS, 1)
            load_w(j - 1, MU, 1)
            if j in (3, 5):
                load_s(j // 2 + 1)
        load_w(NM - 1, MU, 2)

        def t_vec():
            tv = pst.tile([P, NT * P], BF16, tag="tp")
            for t in range(NT):
                nc.tensor.transpose(tv[:, P * t : P * t + P], vec_rows[:, t::NT], ident16[:])
            banks["vec"] = tv

        def e_vec():
            vcopy(
                out=vec[:].rearrange("p (r t) -> p r t", t=NT),
                in_=banks["vec"][:].rearrange("p (t r) -> p r t", t=NT)[:, 0 : 3 * NM, :],
            )

        def noise():
            nc.gpsimd.tensor_copy(out=noise_in[:, 0:NJ], in_=vec[:, 0:NJ])
            nc.gpsimd.tensor_copy(out=noise_in[:, NJ : NJ + NM], in_=ei_in[:])
            nc.vector.scalar_tensor_tensor(
                out=mag[:], in0=noise_in[:], scalar=-1.0, in1=noise_in[:], op0=ALU.mult, op1=ALU.max
            )
            nc.gpsimd.tensor_scalar(out=neg[:], in0=noise_in[:], scalar1=0.0, scalar2=None, op0=ALU.is_lt)
            nc.gpsimd.tensor_scalar(out=sgn[:], in0=noise_in[:], scalar1=0.0, scalar2=None, op0=ALU.is_gt)
            nc.gpsimd.tensor_tensor(out=sgn[:], in0=sgn[:], in1=neg[:], op=ALU.subtract)
            nc.scalar.activation(out=root[:], in_=mag[:], func=ACT.Sqrt)
            nc.scalar.activation(out=warm[:], in_=root[:, 0:1], func=ACT.Exp)
            nc.gpsimd.tensor_tensor(out=f[:], in0=root[:], in1=sgn[:], op=ALU.mult)

        def clip(j):
            a_sb = work.tile([P, 512], F32, tag="a")
            nc.vector.tensor_scalar(
                out=a_sb[:],
                in0=sb[("e", j)][:],
                scalar1=math.exp(-20.0),
                scalar2=math.exp(4.0),
                op0=ALU.max,
                op1=ALU.min,
            )
            sb[("a", j)] = a_sb

        def z_(j):
            z = work.tile([P, 512], F32, tag="z")
            for t in range(NT):
                nc.vector.scalar_tensor_tensor(
                    out=z[:, P * t : P * t + P],
                    in0=sb[("a", j)][:, P * t : P * t + P],
                    scalar=f[:, NT * j + t : NT * j + t + 1],
                    in1=banks[("f", j // 4)][:, P * (j % 4) : P * (j % 4) + P],
                    op0=ALU.mult,
                    op1=ALU.mult,
                )
            sb[("z", j)] = z

        def o_pass(ps, o, first, j, ts):
            for t in ts:
                nc.vector.scalar_tensor_tensor(
                    out=o[:, P * t - first : P * t + P - first],
                    in0=ps[:, P * t : P * t + P],
                    scalar=vec[:, 2 * NJ + NT * j + t : 2 * NJ + NT * j + t + 1],
                    in1=sb[("z", j)][:, P * t : P * t + P],
                    op0=ALU.add,
                    op1=ALU.add,
                )

        def o_(j):
            sb[("o", j)] = work.tile([P, 512], F32, tag="o", name="o")
            o_pass(acc[(MU, j)], sb[("o", j)], 0, j, range(NT))

        make_identity(nc, ident[:])
        nc.vector.memset(warm[:], 1.0)
        nc.scalar.activation(out=warm[:], in_=warm[:], func=ACT.Sqrt)
        vcopy(out=ident16[:], in_=ident[:])
        t_vec()
        t_w(0, LS, 0)
        e_vec()
        noise()
        e_w(0, LS, 0, vcopy)
        t_w(0, LS, 1)
        e_w(0, LS, 1, vcopy)
        t_s(0)
        e_s(0)
        t_w(1, LS, 0)
        t_w(1, LS, 1)
        q_w(0, LS)
        q_s(0)
        t_w(0, MU, 0)
        t_w(0, MU, 1)
        s_at = {0: 1, 2: 2, 4: 3}
        f_at = {0: 0, 4: 1}
        for n in range(NM - 1):
            if n == 0:
                mx(0, LS)
            if n + 1 < NM:
                e_w(n + 1, LS, 0, scopy)
            if 0 <= n - 1 < NM:
                clip(n - 1)
            if n - 1 in s_at:
                q_s(s_at[n - 1])
            if n + 2 < NM:
                t_w(n + 2, LS, 0)
            if 0 <= n - 1 < NM:
                z_(n - 1)
            if n + 1 < NM:
                e_w(n + 1, LS, 1, scopy)
            if n + 2 < NM:
                t_w(n + 2, LS, 1)
            if n == 0:
                x_(0)
            if 0 < n < NM:
                mx(n, LS)
            if 0 <= n - 1 < NM:
                mx(n - 1, MU)
            if n in f_at:
                t_f(f_at[n])
            if n + 1 < NM:
                q_w(n + 1, LS)
            if n in s_at:
                t_s(s_at[n])
            if n in s_at:
                e_s(s_at[n])
            if n < NM:
                e_w(n, MU, 0, scopy)
            if n + 1 < NM:
                t_w(n + 1, MU, 0)
            if n >= 2:
                t_o(n - 2)
            if 0 <= n - 1 < NM:
                o_(n - 1)
            if n < NM:
                e_w(n, MU, 1, scopy)
            if n < NM:
                q_w(n, MU)
            if n + 1 < NM:
                t_w(n + 1, MU, 1)
            if 0 < n < NM:
                x_(n)
            if n >= 2:
                r_(n - 2)
        clip(NM - 2)
        e_w(NM - 1, MU, 0, scopy)
        mx(NM - 1, LS)
        mx(NM - 2, MU)
        t_o(NM - 3)
        z_(NM - 2)
        q_w(NM - 1, MU, 0, 256)
        e_w(NM - 1, MU, 1, scopy)
        x_(NM - 1)
        q_w(NM - 1, MU, 256, 512)
        mx_half(0)
        mx_half(1)
        o_(NM - 2)
        t_o(NM - 2)
        r_(NM - 3)
        clip(NM - 1)
        z_(NM - 1)
        r_(NM - 2)
        o_half(0)
        t_o_half(0)
        o_half(1)
        t_o_half(1)
        r_half(0)
        r_half(1)
